import numpy as np
import ml_dtypes


def mxq(x, axis, fmt="e4m3"):
    dtype, down = {"e4m3": (ml_dtypes.float8_e4m3fn, 7), "e5m2": (ml_dtypes.float8_e5m2, 14)}[fmt]
    v = np.moveaxis(np.asarray(x, np.float32).astype(ml_dtypes.bfloat16).astype(np.float64), axis, -1)
    blocks = v.reshape(v.shape[:-1] + (-1, 32))
    amax = np.abs(blocks).max(-1, keepdims=True)
    byte = np.maximum(np.where(amax > 0, np.frexp(amax)[1] - 1 + 127, 0) - down, 1)
    scale = np.exp2(byte - 127.0)
    codes = (blocks / scale).astype(np.float32).astype(dtype).astype(np.float64)
    return np.moveaxis((codes * scale).reshape(v.shape), -1, axis)


WIDE = False


def mx_kscale(k):
    if not WIDE:
        return np.ones(k)
    levels = np.array([10, -10, 5, -5, 0])
    a = np.random.permutation(np.resize(levels, k // 512 * 4)).reshape(k // 512, 4)
    idx = np.arange(k)
    return np.exp2(a[idx // 512, idx % 128 // 32])


BF16 = ml_dtypes.bfloat16


def bf(x):
    return np.asarray(x, np.float32).astype(BF16)


def f64(x):
    return np.asarray(x).astype(np.float64)


B, S, E, H, KVH, D = 1, 512, 2048, 16, 4, 128


def rope(t, cos, sin):
    tr = t.reshape(t.shape[:-1] + (-1, 2))
    xr, xi = tr[..., 0], tr[..., 1]
    c = cos[None, :, None, :]
    n = sin[None, :, None, :]
    return np.stack([xr * c - xi * n, xr * n + xi * c], axis=-1).reshape(t.shape)


def setup_inputs():
    s = mx_kscale(E)
    a = np.sqrt(2.0 / E)
    ang = np.outer(np.arange(S), 1.0 / (10000.0 ** (np.arange(0, D, 2) / D)))
    return {"x": bf(np.random.standard_normal((B, S, E)) * s),
            "wq_w": bf(np.random.standard_normal((H * D, E)) * a / s[None, :]),
            "wk_w": bf(np.random.standard_normal((KVH * D, E)) * a / s[None, :]),
            "wv_w": bf(np.random.standard_normal((KVH * D, E)) * a / s[None, :]),
            "freqs_cos": bf(np.cos(ang)), "freqs_sin": bf(np.sin(ang))}


def reference(x, wq_w, wk_w, wv_w, freqs_cos, freqs_sin):
    xq = mxq(f64(x), 2, "e4m3")
    q = (xq @ mxq(f64(wq_w), 1, "e4m3").T).reshape(B, S, H, D)
    k = (xq @ mxq(f64(wk_w), 1, "e4m3").T).reshape(B, S, KVH, D)
    v = (xq @ mxq(f64(wv_w), 1, "e4m3").T).reshape(B, S, KVH, D)
    c, n = f64(freqs_cos), f64(freqs_sin)
    return rope(q, c, n), rope(k, c, n), v

@@ -1,0 +1,183 @@
+from contextlib import ExitStack
+
+import concourse.mybir as mybir
+from concourse.masks import make_identity
+
+F32 = mybir.dt.float32
+BF16 = mybir.dt.bfloat16
+U32 = mybir.dt.uint32
+U8 = mybir.dt.uint8
+FP8X4 = mybir.dt.float8_e4m3fn_x4
+MULT = mybir.AluOpType.mult
+ADD = mybir.AluOpType.add
+
+P = 128
+S = 512
+K = 2048
+D = 128
+K_PASS = 4 * P
+PASSES = K // K_PASS
+WORDS_PASS = K_PASS // 2
+HALVES = 2
+ROW_TILES = 2
+BLOCK = ROW_TILES * P
+TOKEN_BLOCKS = S // BLOCK
+TOKEN_TILES = S // P
+HEADS_BLOCK = BLOCK // D
+STORE_COLS = 2 * BLOCK
+
+FLOPS = 2 * S * K * (2048 + 512 + 512)
+
+
+def tile_attention_pa_kernel(
+    tc, x, wq_w, wk_w, wv_w, freqs_cos, freqs_sin, out_0, out_1, out_2
+):
+    nc = tc.nc
+    with ExitStack() as ctx:
+        ctx.enter_context(tc.manual_schedule())
+
+        const = ctx.enter_context(tc.tile_pool(name="const", bufs=1))
+        psum_turn = ctx.enter_context(tc.psum_pool(name="psum_turn", bufs=PASSES))
+        psum_acc = ctx.enter_context(tc.psum_pool(name="psum_acc", bufs=2 * TOKEN_BLOCKS))
+
+        row_blocks = [x[0].rearrange("(p b a) k -> b p (a k)", b=TOKEN_BLOCKS, a=ROW_TILES)[b] for b in range(TOKEN_BLOCKS)]
+        weight_blocks = []
+        for weight, out, rotated in ((wq_w, out_0, True), (wk_w, out_1, True), (wv_w, out_2, False)):
+            out_view = out[0].rearrange("(p m) h d -> p m (h d)", m=TOKEN_TILES)
+            blocks_view = weight.rearrange("(b p a) k -> b p (a k)", p=P, a=ROW_TILES)
+            for b in range(weight.shape[0] // BLOCK):
+                row_blocks.append(blocks_view[b])
+                weight_blocks.append((out_view, b * BLOCK, rotated))
+        n_blocks = len(row_blocks)
+        n_weight_blocks = len(weight_blocks)
+
+        rows_pool = ctx.enter_context(tc.tile_pool(name="rows", bufs=n_blocks))
+        grouped_pool = ctx.enter_context(tc.tile_pool(name="grouped", bufs=3))
+        x_mx_pool = ctx.enter_context(tc.tile_pool(name="x_mx", bufs=TOKEN_BLOCKS))
+        w_mx_pool = ctx.enter_context(tc.tile_pool(name="w_mx", bufs=4))
+        product_pool = ctx.enter_context(tc.tile_pool(name="product", bufs=4))
+        result_pool = ctx.enter_context(tc.tile_pool(name="result", bufs=6))
+
+        rows_sb = []
+        for block_rows in row_blocks:
+            rows = rows_pool.tile([P, ROW_TILES * K], BF16)
+            nc.sync.dma_start(out=rows[:], in_=block_rows)
+            rows_sb.append(rows)
+
+        ident = const.tile([P, P], F32)
+        make_identity(nc, ident[:])
+        cos_sb = const.tile([P, TOKEN_TILES, D // 2], BF16)
+        sin_sb = const.tile([P, TOKEN_TILES, D // 2], BF16)
+        nc.scalar.dma_start(out=cos_sb[:], in_=freqs_cos.rearrange("(p m) j -> p m j", m=TOKEN_TILES))
+        nc.scalar.dma_start(out=sin_sb[:], in_=freqs_sin.rearrange("(p m) j -> p m j", m=TOKEN_TILES))
+        for_even = const.tile([P, TOKEN_TILES, D // 2, 2], F32)
+        for_odd = const.tile([P, TOKEN_TILES, D // 2, 2], F32)
+        nc.vector.tensor_copy(out=for_even[:, :, :, 0:1], in_=cos_sb[:].unsqueeze(3))
+        nc.vector.tensor_copy(out=for_even[:, :, :, 1:2], in_=sin_sb[:].unsqueeze(3))
+        nc.vector.tensor_scalar_mul(out=for_odd[:, :, :, 0:1], in0=sin_sb[:].unsqueeze(3), scalar1=-1.0)
+        nc.vector.tensor_copy(out=for_odd[:, :, :, 1:2], in_=cos_sb[:].unsqueeze(3))
+
+        def turn_block(rows):
+            words = rows[:].bitcast(F32)
+            grouped = grouped_pool.tile([P, PASSES * BLOCK * 4], BF16, align_bytes=64)
+            grouped_words = grouped[:].bitcast(F32)
+            for g in range(PASSES):
+                bank = psum_turn.tile([P, ROW_TILES, HALVES, P], F32)
+                for a in range(ROW_TILES):
+                    for u in range(HALVES):
+                        first = a * (K // 2) + g * WORDS_PASS + u * P
+                        nc.tensor.transpose(bank[:, a, u, :], words[:, first : first + P], ident[:])
+                nc.scalar.copy(
+                    out=grouped_words[:, g * BLOCK * HALVES : (g + 1) * BLOCK * HALVES].rearrange(
+                        "p (a r u) -> p a r u", a=ROW_TILES, u=HALVES
+                    ),
+                    in_=bank[:].rearrange("p a u r -> p a r u"),
+                )
+            return grouped
+
+        def quantise_block(pool, grouped):
+            codes = pool.tile([P, PASSES * BLOCK], U32, align_bytes=64)
+            scales = pool.tile([P, PASSES * BLOCK], U8, align_bytes=64)
+            nc.vector.quantize_mx(out=codes[:].bitcast(FP8X4), scales=scales[:], in_=grouped[:])
+            return codes, scales
+
+        def multiply_block(x_mx, w_mx):
+            w_codes, w_scales = w_mx
+            banks = []
+            for x_codes, x_scales in x_mx:
+                acc = psum_acc.tile([P, ROW_TILES * BLOCK], F32)
+                for a in range(ROW_TILES):
+                    for g in range(PASSES):
+                        tokens = slice(g * BLOCK + a * P, g * BLOCK + (a + 1) * P)
+                        features = slice(g * BLOCK, (g + 1) * BLOCK)
+                        nc.tensor.matmul_mx(
+                            out=acc[:, a * BLOCK : (a + 1) * BLOCK],
+                            lhsT=x_codes[:, tokens].bitcast(FP8X4),
+                            lhsT_scale=x_scales[:, tokens],
+                            rhs=w_codes[:, features].bitcast(FP8X4),
+                            rhs_scale=w_scales[:, features],
+                            start=(g == 0),
+                            stop=(g == PASSES - 1),
+                        )
+                banks.append(acc)
+            return banks
+
+        pair_shape = [P, ROW_TILES, HEADS_BLOCK, D // 2, 2]
+
+        def rotate_bank(acc, token_block):
+            planes = acc[:].rearrange("p (m e h j) -> p m e h j", m=ROW_TILES, e=2, h=HEADS_BLOCK)
+            tiles = slice(token_block * ROW_TILES, (token_block + 1) * ROW_TILES)
+            products = []
+            for e, table in enumerate((for_even, for_odd)):
+                product = product_pool.tile([P, ROW_TILES, BLOCK], F32, name="product%d" % e)
+                nc.vector.tensor_tensor(
+                    out=product[:].rearrange("p m (h j e) -> p m h j e", h=HEADS_BLOCK, e=2),
+                    in0=planes[:, :, e : e + 1].rearrange("p m o h j -> p m h j o").to_broadcast(pair_shape),
+                    in1=table[:, tiles].unsqueeze(2).to_broadcast(pair_shape),
+                    op=MULT,
+                )
+                products.append(product)
+            return products
+
+        results = {}
+
+        def finish_block(w, banks):
+            out_view, first_col, rotated = weight_blocks[w]
+            store_first = first_col // STORE_COLS * STORE_COLS
+            cols = slice(first_col - store_first, first_col - store_first + BLOCK)
+            if first_col == store_first:
+                for t in range(TOKEN_BLOCKS):
+                    results[t] = result_pool.tile([P, ROW_TILES, STORE_COLS], F32, name="result")
+            if rotated:
+                products = [rotate_bank(banks[t], t) for t in range(TOKEN_BLOCKS)]
+                for t in range(TOKEN_BLOCKS):
+                    nc.vector.tensor_tensor(
+                        out=results[t][:, :, cols], in0=products[t][0][:], in1=products[t][1][:], op=ADD
+                    )
+            else:
+                for t in range(TOKEN_BLOCKS):
+                    nc.scalar.copy(
+                        out=results[t][:, :, cols].rearrange("p m (r e) -> p m r e", e=2),
+                        in_=banks[t][:].rearrange("p (m e r) -> p m r e", m=ROW_TILES, e=2),
+                    )
+            if first_col + BLOCK == store_first + STORE_COLS:
+                for t in range(TOKEN_BLOCKS):
+                    nc.sync.dma_start(
+                        out=out_view[:, t * ROW_TILES : (t + 1) * ROW_TILES, store_first : store_first + STORE_COLS],
+                        in_=results[t][:],
+                    )
+
+        grouped = {}
+        mx = {}
+        banks = {}
+        for step in range(n_blocks + 3):
+            if step < n_blocks:
+                grouped[step] = turn_block(rows_sb[step])
+            if 0 <= step - 1 < n_blocks:
+                pool = x_mx_pool if step - 1 < TOKEN_BLOCKS else w_mx_pool
+                mx[step - 1] = quantise_block(pool, grouped[step - 1])
+            w = step - 2 - TOKEN_BLOCKS
+            if 0 <= w < n_weight_blocks:
+                banks[w] = multiply_block([mx[t] for t in range(TOKEN_BLOCKS)], mx[w + TOKEN_BLOCKS])
+            if 0 <= w - 1 < n_weight_blocks:
+                finish_block(w - 1, banks[w - 1])

@@ -151,7 +151,7 @@ def tile_attention_pa_kernel(
             if rotated:
                 products = [rotate_bank(banks[t], t) for t in range(TOKEN_BLOCKS)]
                 for t in range(TOKEN_BLOCKS):
-                    nc.vector.tensor_tensor(
+                    nc.gpsimd.tensor_tensor(
                         out=results[t][:, :, cols], in0=products[t][0][:], in1=products[t][1][:], op=ADD
                     )
             else:

@@ -70,12 +70,11 @@ def tile_attention_pa_kernel(
         sin_sb = const.tile([P, TOKEN_TILES, D // 2], BF16)
         nc.scalar.dma_start(out=cos_sb[:], in_=freqs_cos.rearrange("(p m) j -> p m j", m=TOKEN_TILES))
         nc.scalar.dma_start(out=sin_sb[:], in_=freqs_sin.rearrange("(p m) j -> p m j", m=TOKEN_TILES))
-        for_even = const.tile([P, TOKEN_TILES, D // 2, 2], F32)
-        for_odd = const.tile([P, TOKEN_TILES, D // 2, 2], F32)
-        nc.vector.tensor_copy(out=for_even[:, :, :, 0:1], in_=cos_sb[:].unsqueeze(3))
-        nc.vector.tensor_copy(out=for_even[:, :, :, 1:2], in_=sin_sb[:].unsqueeze(3))
-        nc.vector.tensor_scalar_mul(out=for_odd[:, :, :, 0:1], in0=sin_sb[:].unsqueeze(3), scalar1=-1.0)
-        nc.vector.tensor_copy(out=for_odd[:, :, :, 1:2], in_=cos_sb[:].unsqueeze(3))
+        factors = const.tile([P, TOKEN_TILES, 2, D // 2, 2], F32)
+        nc.vector.tensor_copy(out=factors[:, :, 0, :, 0:1], in_=cos_sb[:].unsqueeze(3))
+        nc.vector.tensor_copy(out=factors[:, :, 0, :, 1:2], in_=sin_sb[:].unsqueeze(3))
+        nc.vector.tensor_scalar_mul(out=factors[:, :, 1, :, 0:1], in0=sin_sb[:].unsqueeze(3), scalar1=-1.0)
+        nc.vector.tensor_copy(out=factors[:, :, 1, :, 1:2], in_=cos_sb[:].unsqueeze(3))
 
         def turn_block(rows):
             words = rows[:].bitcast(F32)
@@ -122,22 +121,21 @@ def tile_attention_pa_kernel(
                 banks.append(acc)
             return banks
 
-        pair_shape = [P, ROW_TILES, HEADS_BLOCK, D // 2, 2]
+        product_shape = [P, ROW_TILES, 2, HEADS_BLOCK, D // 2, 2]
 
-        def rotate_bank(acc, token_block):
-            planes = acc[:].rearrange("p (m e h j) -> p m e h j", m=ROW_TILES, e=2, h=HEADS_BLOCK)
+        def multiply_by_factors(acc, token_block):
             tiles = slice(token_block * ROW_TILES, (token_block + 1) * ROW_TILES)
-            products = []
-            for e, table in enumerate((for_even, for_odd)):
-                product = product_pool.tile([P, ROW_TILES, BLOCK], F32, name="product%d" % e)
-                nc.vector.tensor_tensor(
-                    out=product[:].rearrange("p m (h j e) -> p m h j e", h=HEADS_BLOCK, e=2),
-                    in0=planes[:, :, e : e + 1].rearrange("p m o h j -> p m h j o").to_broadcast(pair_shape),
-                    in1=table[:, tiles].unsqueeze(2).to_broadcast(pair_shape),
-                    op=MULT,
-                )
-                products.append(product)
-            return products
+            product = product_pool.tile([P, ROW_TILES, 2, BLOCK], F32)
+            nc.vector.tensor_tensor(
+                out=product[:].rearrange("p m w (h j e) -> p m w h j e", h=HEADS_BLOCK, e=2),
+                in0=acc[:]
+                .rearrange("p (m w h j) -> p m w h j", m=ROW_TILES, w=2, h=HEADS_BLOCK)
+                .unsqueeze(5)
+                .to_broadcast(product_shape),
+                in1=factors[:, tiles].unsqueeze(3).to_broadcast(product_shape),
+                op=MULT,
+            )
+            return product
 
         results = {}
 
@@ -149,10 +147,10 @@ def tile_attention_pa_kernel(
                 for t in range(TOKEN_BLOCKS):
                     results[t] = result_pool.tile([P, ROW_TILES, STORE_COLS], F32, name="result")
             if rotated:
-                products = [rotate_bank(banks[t], t) for t in range(TOKEN_BLOCKS)]
+                products = [multiply_by_factors(banks[t], t) for t in range(TOKEN_BLOCKS)]
                 for t in range(TOKEN_BLOCKS):
                     nc.gpsimd.tensor_tensor(
-                        out=results[t][:, :, cols], in0=products[t][0][:], in1=products[t][1][:], op=ADD
+                        out=results[t][:, :, cols], in0=products[t][:, :, 0, :], in1=products[t][:, :, 1, :], op=ADD
                     )
             else:
                 for t in range(TOKEN_BLOCKS):

@@ -24,7 +24,6 @@ BLOCK = ROW_TILES * P
 TOKEN_BLOCKS = S // BLOCK
 TOKEN_TILES = S // P
 HEADS_BLOCK = BLOCK // D
-STORE_COLS = 2 * BLOCK
 
 FLOPS = 2 * S * K * (2048 + 512 + 512)
 
@@ -137,33 +136,24 @@ def tile_attention_pa_kernel(
             )
             return product
 
-        results = {}
-
         def finish_block(w, banks):
             out_view, first_col, rotated = weight_blocks[w]
-            store_first = first_col // STORE_COLS * STORE_COLS
-            cols = slice(first_col - store_first, first_col - store_first + BLOCK)
-            if first_col == store_first:
-                for t in range(TOKEN_BLOCKS):
-                    results[t] = result_pool.tile([P, ROW_TILES, STORE_COLS], F32, name="result")
-            if rotated:
-                products = [multiply_by_factors(banks[t], t) for t in range(TOKEN_BLOCKS)]
-                for t in range(TOKEN_BLOCKS):
+            for t, acc in enumerate(banks):
+                result = result_pool.tile([P, ROW_TILES, BLOCK], F32)
+                if rotated:
+                    product = multiply_by_factors(acc, t)
                     nc.gpsimd.tensor_tensor(
-                        out=results[t][:, :, cols], in0=products[t][:, :, 0, :], in1=products[t][:, :, 1, :], op=ADD
+                        out=result[:], in0=product[:, :, 0, :], in1=product[:, :, 1, :], op=ADD
                     )
-            else:
-                for t in range(TOKEN_BLOCKS):
+                else:
                     nc.scalar.copy(
-                        out=results[t][:, :, cols].rearrange("p m (r e) -> p m r e", e=2),
-                        in_=banks[t][:].rearrange("p (m e r) -> p m r e", m=ROW_TILES, e=2),
+                        out=result[:].rearrange("p m (r e) -> p m r e", e=2),
+                        in_=acc[:].rearrange("p (m e r) -> p m r e", m=ROW_TILES, e=2),
                     )
-            if first_col + BLOCK == store_first + STORE_COLS:
-                for t in range(TOKEN_BLOCKS):
-                    nc.sync.dma_start(
-                        out=out_view[:, t * ROW_TILES : (t + 1) * ROW_TILES, store_first : store_first + STORE_COLS],
-                        in_=results[t][:],
-                    )
+                nc.sync.dma_start(
+                    out=out_view[:, t * ROW_TILES : (t + 1) * ROW_TILES, first_col : first_col + BLOCK],
+                    in_=result[:],
+                )
 
         grouped = {}
         mx = {}

from contextlib import ExitStack

import concourse.mybir as mybir
from concourse.masks import make_identity

F32 = mybir.dt.float32
BF16 = mybir.dt.bfloat16
U32 = mybir.dt.uint32
U8 = mybir.dt.uint8
FP8X4 = mybir.dt.float8_e4m3fn_x4
MULT = mybir.AluOpType.mult
ADD = mybir.AluOpType.add

P = 128
S = 512
K = 2048
D = 128
K_PASS = 4 * P
PASSES = K // K_PASS
WORDS_PASS = K_PASS // 2
HALVES = 2
ROW_TILES = 2
BLOCK = ROW_TILES * P
TOKEN_BLOCKS = S // BLOCK
TOKEN_TILES = S // P
HEADS_BLOCK = BLOCK // D

FLOPS = 2 * S * K * (2048 + 512 + 512)


def tile_attention_pa_kernel(
    tc, x, wq_w, wk_w, wv_w, freqs_cos, freqs_sin, out_0, out_1, out_2
):
    nc = tc.nc
    with ExitStack() as ctx:
        ctx.enter_context(tc.manual_schedule())

        const = ctx.enter_context(tc.tile_pool(name="const", bufs=1))
        psum_turn = ctx.enter_context(tc.psum_pool(name="psum_turn", bufs=PASSES))
        psum_acc = ctx.enter_context(tc.psum_pool(name="psum_acc", bufs=2 * TOKEN_BLOCKS))

        row_blocks = [x[0].rearrange("(p b a) k -> b p (a k)", b=TOKEN_BLOCKS, a=ROW_TILES)[b] for b in range(TOKEN_BLOCKS)]
        weight_blocks = []
        for weight, out, rotated in ((wq_w, out_0, True), (wk_w, out_1, True), (wv_w, out_2, False)):
            out_view = out[0].rearrange("(p m) h d -> p m (h d)", m=TOKEN_TILES)
            blocks_view = weight.rearrange("(b p a) k -> b p (a k)", p=P, a=ROW_TILES)
            for b in range(weight.shape[0] // BLOCK):
                row_blocks.append(blocks_view[b])
                weight_blocks.append((out_view, b * BLOCK, rotated))
        n_blocks = len(row_blocks)
        n_weight_blocks = len(weight_blocks)

        rows_pool = ctx.enter_context(tc.tile_pool(name="rows", bufs=n_blocks))
        grouped_pool = ctx.enter_context(tc.tile_pool(name="grouped", bufs=3))
        x_mx_pool = ctx.enter_context(tc.tile_pool(name="x_mx", bufs=TOKEN_BLOCKS))
        w_mx_pool = ctx.enter_context(tc.tile_pool(name="w_mx", bufs=4))
        product_pool = ctx.enter_context(tc.tile_pool(name="product", bufs=4))
        result_pool = ctx.enter_context(tc.tile_pool(name="result", bufs=6))

        rows_sb = []
        for block_rows in row_blocks:
            rows = rows_pool.tile([P, ROW_TILES * K], BF16)
            nc.sync.dma_start(out=rows[:], in_=block_rows)
            rows_sb.append(rows)

        ident = const.tile([P, P], F32)
        make_identity(nc, ident[:])
        cos_sb = const.tile([P, TOKEN_TILES, D // 2], BF16)
        sin_sb = const.tile([P, TOKEN_TILES, D // 2], BF16)
        nc.scalar.dma_start(out=cos_sb[:], in_=freqs_cos.rearrange("(p m) j -> p m j", m=TOKEN_TILES))
        nc.scalar.dma_start(out=sin_sb[:], in_=freqs_sin.rearrange("(p m) j -> p m j", m=TOKEN_TILES))
        factors = const.tile([P, TOKEN_TILES, 2, D // 2, 2], F32)
        nc.vector.tensor_copy(out=factors[:, :, 0, :, 0:1], in_=cos_sb[:].unsqueeze(3))
        nc.vector.tensor_copy(out=factors[:, :, 0, :, 1:2], in_=sin_sb[:].unsqueeze(3))
        nc.vector.tensor_scalar_mul(out=factors[:, :, 1, :, 0:1], in0=sin_sb[:].unsqueeze(3), scalar1=-1.0)
        nc.vector.tensor_copy(out=factors[:, :, 1, :, 1:2], in_=cos_sb[:].unsqueeze(3))

        def turn_block(rows):
            words = rows[:].bitcast(F32)
            grouped = grouped_pool.tile([P, PASSES * BLOCK * 4], BF16, align_bytes=64)
            grouped_words = grouped[:].bitcast(F32)
            for g in range(PASSES):
                bank = psum_turn.tile([P, ROW_TILES, HALVES, P], F32)
                for a in range(ROW_TILES):
                    for u in range(HALVES):
                        first = a * (K // 2) + g * WORDS_PASS + u * P
                        nc.tensor.transpose(bank[:, a, u, :], words[:, first : first + P], ident[:])
                nc.scalar.copy(
                    out=grouped_words[:, g * BLOCK * HALVES : (g + 1) * BLOCK * HALVES].rearrange(
                        "p (a r u) -> p a r u", a=ROW_TILES, u=HALVES
                    ),
                    in_=bank[:].rearrange("p a u r -> p a r u"),
                )
            return grouped

        def quantise_block(pool, grouped):
            codes = pool.tile([P, PASSES * BLOCK], U32, align_bytes=64)
            scales = pool.tile([P, PASSES * BLOCK], U8, align_bytes=64)
            nc.vector.quantize_mx(out=codes[:].bitcast(FP8X4), scales=scales[:], in_=grouped[:])
            return codes, scales

        def multiply_block(x_mx, w_mx):
            w_codes, w_scales = w_mx
            banks = []
            for x_codes, x_scales in x_mx:
                acc = psum_acc.tile([P, ROW_TILES * BLOCK], F32)
                for a in range(ROW_TILES):
                    for g in range(PASSES):
                        tokens = slice(g * BLOCK + a * P, g * BLOCK + (a + 1) * P)
                        features = slice(g * BLOCK, (g + 1) * BLOCK)
                        nc.tensor.matmul_mx(
                            out=acc[:, a * BLOCK : (a + 1) * BLOCK],
                            lhsT=x_codes[:, tokens].bitcast(FP8X4),
                            lhsT_scale=x_scales[:, tokens],
                            rhs=w_codes[:, features].bitcast(FP8X4),
                            rhs_scale=w_scales[:, features],
                            start=(g == 0),
                            stop=(g == PASSES - 1),
                        )
                banks.append(acc)
            return banks

        product_shape = [P, ROW_TILES, 2, HEADS_BLOCK, D // 2, 2]

        def multiply_by_factors(acc, token_block):
            tiles = slice(token_block * ROW_TILES, (token_block + 1) * ROW_TILES)
            product = product_pool.tile([P, ROW_TILES, 2, BLOCK], F32)
            nc.vector.tensor_tensor(
                out=product[:].rearrange("p m w (h j e) -> p m w h j e", h=HEADS_BLOCK, e=2),
                in0=acc[:]
                .rearrange("p (m w h j) -> p m w h j", m=ROW_TILES, w=2, h=HEADS_BLOCK)
                .unsqueeze(5)
                .to_broadcast(product_shape),
                in1=factors[:, tiles].unsqueeze(3).to_broadcast(product_shape),
                op=MULT,
            )
            return product

        def finish_block(w, banks):
            out_view, first_col, rotated = weight_blocks[w]
            for t, acc in enumerate(banks):
                result = result_pool.tile([P, ROW_TILES, BLOCK], F32)
                if rotated:
                    product = multiply_by_factors(acc, t)
                    nc.gpsimd.tensor_tensor(
                        out=result[:], in0=product[:, :, 0, :], in1=product[:, :, 1, :], op=ADD
                    )
                else:
                    nc.scalar.copy(
                        out=result[:].rearrange("p m (r e) -> p m r e", e=2),
                        in_=acc[:].rearrange("p (m e r) -> p m r e", m=ROW_TILES, e=2),
                    )
                nc.sync.dma_start(
                    out=out_view[:, t * ROW_TILES : (t + 1) * ROW_TILES, first_col : first_col + BLOCK],
                    in_=result[:],
                )

        grouped = {}
        mx = {}
        banks = {}
        for step in range(n_blocks + 3):
            if step < n_blocks:
                grouped[step] = turn_block(rows_sb[step])
            if 0 <= step - 1 < n_blocks:
                pool = x_mx_pool if step - 1 < TOKEN_BLOCKS else w_mx_pool
                mx[step - 1] = quantise_block(pool, grouped[step - 1])
            w = step - 2 - TOKEN_BLOCKS
            if 0 <= w < n_weight_blocks:
                banks[w] = multiply_block([mx[t] for t in range(TOKEN_BLOCKS)], mx[w + TOKEN_BLOCKS])
            if 0 <= w - 1 < n_weight_blocks:
                finish_block(w - 1, banks[w - 1])
